import numpy as np
import ml_dtypes


def mxq(x, axis, fmt="e4m3"):
    dtype, down = {"e4m3": (ml_dtypes.float8_e4m3fn, 7), "e5m2": (ml_dtypes.float8_e5m2, 14)}[fmt]
    v = np.moveaxis(np.asarray(x, np.float32).astype(ml_dtypes.bfloat16).astype(np.float64), axis, -1)
    blocks = v.reshape(v.shape[:-1] + (-1, 32))
    amax = np.abs(blocks).max(-1, keepdims=True)
    byte = np.maximum(np.where(amax > 0, np.frexp(amax)[1] - 1 + 127, 0) - down, 1)
    scale = np.exp2(byte - 127.0)
    codes = (blocks / scale).astype(np.float32).astype(dtype).astype(np.float64)
    return np.moveaxis((codes * scale).reshape(v.shape), -1, axis)


WIDE = False


def mx_kscale(k):
    if not WIDE:
        return np.ones(k)
    levels = np.array([10, -10, 5, -5, 0])
    a = np.random.permutation(np.resize(levels, k // 512 * 4)).reshape(k // 512, 4)
    idx = np.arange(k)
    return np.exp2(a[idx // 512, idx % 128 // 32])


BF16 = ml_dtypes.bfloat16


def bf(x):
    return np.asarray(x, np.float32).astype(BF16)


def f64(x):
    return np.asarray(x).astype(np.float64)


B, IN, HID, PROJ, H, KC = 8192, 512, 128, 128, 4, 4
EPS = 1e-5


def silu(v):
    return v / (1.0 + np.exp(-v))


def layernorm(v, w, b):
    mu = v.mean(-1, keepdims=True)
    var = ((v - mu) ** 2).mean(-1, keepdims=True)
    return (v - mu) / np.sqrt(var + EPS) * w + b


def causal_conv(v, w, b):
    vp = np.pad(v, ((0, 0), (KC - 1, 0)))
    L = v.shape[1]
    return b + sum(w[j] * vp[:, j:j + L] for j in range(KC))


def setup_inputs():
    s = mx_kscale(IN)
    r = np.random.standard_normal
    return {"x": bf(r((B, IN))),
            "ln_w": bf((1.0 + 0.1 * r(IN)) * s), "ln_b": bf(0.1 * r(IN) * s),
            "upL_w": bf(r((IN, PROJ)) / np.sqrt(IN) / s[:, None]), "upL_b": bf(0.2 * r(PROJ)),
            "upR_w": bf(r((IN, HID)) / np.sqrt(IN) / s[:, None]), "upR_b": bf(0.2 * r(HID)),
            "conv_w": bf((1.0 + 0.3 * r(KC)) / np.sqrt(KC)), "conv_b": bf(0.2 + 0.1 * r(1))}


def reference(x, ln_w, ln_b, upL_w, upL_b, upR_w, upR_b, conv_w, conv_b):
    xn = mxq(layernorm(f64(x), f64(ln_w), f64(ln_b)), 1, "e4m3")
    x_left = (xn @ mxq(f64(upL_w), 0, "e4m3")) + f64(upL_b)
    x_right = (xn @ mxq(f64(upR_w), 0, "e4m3")) + f64(upR_b)
    x_conv = silu(causal_conv(x_left, f64(conv_w), f64(conv_b)))
    return x_left, x_conv, x_right

@@ -1,0 +1,249 @@
+from contextlib import ExitStack
+
+import concourse.mybir as mybir
+from concourse.masks import make_identity
+
+F32 = mybir.dt.float32
+BF16 = mybir.dt.bfloat16
+U32 = mybir.dt.uint32
+U8 = mybir.dt.uint8
+FP8X4 = mybir.dt.float8_e4m3fn_x4
+ALU = mybir.AluOpType
+ACT = mybir.ActivationFunctionType
+
+P = 128
+PACK = 4
+ROWS, IN, FEAT, TAPS = 8192, 512, 128, 4
+EPS = 1e-5
+SUB = 4
+GROUP_ROWS = P * SUB
+N_GROUPS = ROWS // GROUP_ROWS
+STATS_LEAD = 3
+
+FLOPS = 2 * ROWS * IN * 2 * FEAT
+
+
+def tile_mlstmblock_pa_t_kernel(
+    tc, x, ln_w, ln_b, upL_w, upL_b, upR_w, upR_b, conv_w, conv_b, out_0, out_1, out_2
+):
+    nc = tc.nc
+    with ExitStack() as ctx:
+        const = ctx.enter_context(tc.tile_pool(name="const", bufs=1))
+        xin = ctx.enter_context(tc.tile_pool(name="xin", bufs=1))
+        small = ctx.enter_context(tc.tile_pool(name="small", bufs=STATS_LEAD + 3))
+        work = ctx.enter_context(tc.tile_pool(name="work", bufs=3))
+        tpsum = ctx.enter_context(tc.psum_pool(name="tpsum", bufs=1))
+        mpsum = ctx.enter_context(tc.psum_pool(name="mpsum", bufs=4))
+        ctx.enter_context(tc.manual_schedule())
+
+        def group_rows(dram, g):
+            return dram[g * GROUP_ROWS : (g + 1) * GROUP_ROWS, :].rearrange(
+                "(p j) n -> p j n", j=SUB
+            )
+
+        vec_rows = const.tile([P, P], BF16, name="vec_rows")
+        nc.vector.memset(vec_rows[:], 0.0)
+        x_sb = [xin.tile([P, SUB, IN], BF16, name="x%d" % g) for g in range(N_GROUPS)]
+        for g in range(N_GROUPS):
+            nc.sync.dma_start(out=x_sb[g][:], in_=group_rows(x, g))
+        nc.scalar.dma_start(out=vec_rows[0:PACK, :], in_=ln_w.rearrange("(c p) -> c p", p=P))
+        nc.scalar.dma_start(
+            out=vec_rows[PACK : 2 * PACK, :], in_=ln_b.rearrange("(c p) -> c p", p=P)
+        )
+        w_raw = const.tile([P, PACK, 2 * FEAT], BF16, name="w_raw")
+        nc.scalar.dma_start(
+            out=w_raw[:, :, 0:FEAT], in_=upL_w.rearrange("(c p) n -> p c n", p=P)
+        )
+        nc.scalar.dma_start(
+            out=w_raw[:, :, FEAT : 2 * FEAT], in_=upR_w.rearrange("(c p) n -> p c n", p=P)
+        )
+        bias_bf = const.tile([P, 2 * FEAT], BF16, name="bias_bf")
+        nc.scalar.dma_start(out=bias_bf[:, 0:FEAT], in_=upL_b.partition_broadcast(P))
+        nc.scalar.dma_start(out=bias_bf[:, FEAT : 2 * FEAT], in_=upR_b.partition_broadcast(P))
+        taps_bf = const.tile([P, TAPS], BF16, name="taps_bf")
+        nc.scalar.dma_start(out=taps_bf[:], in_=conv_w.partition_broadcast(P))
+        cbias_bf = const.tile([P, 1], BF16, name="cbias_bf")
+        nc.scalar.dma_start(out=cbias_bf[:], in_=conv_b.partition_broadcast(P))
+
+        ident = const.tile([P, P], F32, name="ident")
+        make_identity(nc, ident[:])
+        neg_half = const.tile([P, SUB], F32, name="neg_half")
+        nc.gpsimd.memset(neg_half[:], -0.5)
+
+        mean_var = {}
+        normed = {}
+        grouped = {}
+        outs = {}
+        conv_acc = {}
+
+        def stats(g):
+            mv = small.tile([P, SUB, 2], F32, name="mv")
+            for j in range(SUB):
+                st = small.tile([P, 6], F32, name="st")
+                nc.vector.bn_stats(out=st[:], in_=x_sb[g][:, j, :])
+                nc.vector.bn_aggr(out=mv[:, j, :], in_=st[:])
+            mean_var[g] = mv
+
+        def constants():
+            vec_rows32 = const.tile([P, P], F32, name="vec_rows32")
+            nc.vector.tensor_copy(out=vec_rows32[:], in_=vec_rows[:])
+            vec_ps = tpsum.tile([P, GROUP_ROWS], F32, name="vec_ps", tag="tp0")
+            nc.tensor.transpose(out=vec_ps[:, 0:P], in_=vec_rows32[:], identity=ident[:])
+            ln_cols = const.tile([P, 2 * PACK], F32, name="ln_cols")
+            nc.vector.tensor_copy(out=ln_cols[:], in_=vec_ps[:, 0 : 2 * PACK])
+            w_grouped = const.tile([P, 2 * FEAT, PACK], BF16, name="w_grouped", align_bytes=64)
+            nc.vector.tensor_copy(out=w_grouped[:], in_=w_raw[:].rearrange("p c n -> p n c"))
+            w_codes = const.tile([P, 2 * FEAT], U32, name="w_codes", align_bytes=64)
+            w_scales = const.tile([P, 2 * FEAT], U8, name="w_scales", align_bytes=64)
+            bias_bc = const.tile([P, 2 * FEAT], F32, name="bias_bc")
+            nc.vector.tensor_copy(out=bias_bc[:], in_=bias_bf[:])
+            nc.vector.quantize_mx(
+                out=w_codes[:].bitcast(FP8X4),
+                scales=w_scales[:],
+                in_=w_grouped[:].rearrange("p n c -> p (n c)"),
+            )
+            taps = const.tile([P, TAPS], F32, name="taps")
+            nc.vector.tensor_copy(out=taps[:], in_=taps_bf[:])
+            cbias = const.tile([P, 1], F32, name="cbias")
+            nc.vector.tensor_copy(out=cbias[:], in_=cbias_bf[:])
+            return ln_cols, w_codes, w_scales, bias_bc, taps, cbias
+
+        def normalise(g):
+            mv = mean_var.pop(g)
+            var_eps = small.tile([P, SUB], F32, name="var_eps")
+            nc.gpsimd.tensor_scalar(
+                out=var_eps[:], in0=mv[:, :, 1], scalar1=1.0, scalar2=EPS, op0=ALU.mult, op1=ALU.add
+            )
+            rstd = small.tile([P, SUB], F32, name="rstd")
+            nc.gpsimd.tensor_tensor(out=rstd[:], in0=var_eps[:], in1=neg_half[:], op=ALU.pow)
+            neg_mean = small.tile([P, SUB], F32, name="neg_mean")
+            nc.gpsimd.tensor_scalar(
+                out=neg_mean[:], in0=mv[:, :, 0], scalar1=-1.0, scalar2=0.0, op0=ALU.mult, op1=ALU.add
+            )
+            t = work.tile([P, SUB, IN], F32, name="t")
+            for j in range(SUB):
+                nc.gpsimd.tensor_scalar(
+                    out=t[:, j, :],
+                    in0=x_sb[g][:, j, :],
+                    scalar1=neg_mean[:, j : j + 1],
+                    scalar2=rstd[:, j : j + 1],
+                    op0=ALU.add,
+                    op1=ALU.mult,
+                )
+            normed[g] = t
+
+        def transpose_and_scale(g):
+            t = normed.pop(g)
+            planes = work.tile([P, PACK, GROUP_ROWS], BF16, name="planes")
+            banks = []
+            for c in range(PACK):
+                bank = tpsum.tile([P, GROUP_ROWS], F32, name="bank", tag="tp%d" % c)
+                for j in range(SUB):
+                    nc.tensor.transpose(
+                        out=bank[:, j * P : (j + 1) * P],
+                        in_=t[:, j, c * P : (c + 1) * P],
+                        identity=ident[:],
+                    )
+                banks.append(bank)
+            for c in range(PACK):
+                nc.scalar.activation(
+                    out=planes[:, c, :],
+                    in_=banks[c][:],
+                    func=ACT.Identity,
+                    scale=ln_cols[:, c : c + 1],
+                    bias=ln_cols[:, PACK + c : PACK + c + 1],
+                )
+            grp = work.tile([P, GROUP_ROWS, PACK], BF16, name="grp", align_bytes=64)
+            nc.scalar.copy(out=grp[:], in_=planes[:].rearrange("p c r -> p r c"))
+            grouped[g] = grp
+
+        def project(g):
+            grp = grouped.pop(g)
+            codes = work.tile([P, GROUP_ROWS], U32, name="codes", align_bytes=64)
+            scales = work.tile([P, GROUP_ROWS], U8, name="scales", align_bytes=64)
+            nc.vector.quantize_mx(
+                out=codes[:].bitcast(FP8X4),
+                scales=scales[:],
+                in_=grp[:].rearrange("p r c -> p (r c)"),
+            )
+            banks = []
+            for h in range(SUB // 2):
+                acc = mpsum.tile([P, 2, 2 * FEAT], F32, name="acc")
+                for i in range(2):
+                    cols = slice((2 * h + i) * P, (2 * h + i + 1) * P)
+                    nc.tensor.matmul_mx(
+                        out=acc[:, i, :],
+                        lhsT=codes[:, cols].bitcast(FP8X4),
+                        lhsT_scale=scales[:, cols],
+                        rhs=w_codes[:].bitcast(FP8X4),
+                        rhs_scale=w_scales[:],
+                        start=True,
+                        stop=True,
+                    )
+                banks.append(acc)
+            return banks
+
+        def add_bias(g, banks):
+            o = work.tile([P, 2, SUB, FEAT], F32, name="o")
+            for h in range(SUB // 2):
+                nc.vector.tensor_tensor(
+                    out=o[:, :, 2 * h : 2 * h + 2, :].rearrange("p l j n -> p j l n"),
+                    in0=banks[h][:].rearrange("p j (l n) -> p j l n", l=2),
+                    in1=bias_bc[:]
+                    .rearrange("p (l n) -> p l n", l=2)
+                    .unsqueeze(1)
+                    .to_broadcast([P, 2, 2, FEAT]),
+                    op=ALU.add,
+                )
+            nc.sync.dma_start(out=group_rows(out_0, g), in_=o[:, 0, :, :])
+            nc.sync.dma_start(out=group_rows(out_2, g), in_=o[:, 1, :, :])
+            cv = work.tile([P, SUB, FEAT], F32, name="cv")
+            nc.gpsimd.tensor_scalar(
+                out=cv[:],
+                in0=o[:, 0, :, :],
+                scalar1=taps[:, TAPS - 1 : TAPS],
+                scalar2=cbias[:, 0:1],
+                op0=ALU.mult,
+                op1=ALU.add,
+            )
+            outs[g] = o
+            conv_acc[g] = cv
+
+        def convolve(g):
+            o = outs.pop(g)
+            cv = conv_acc[g]
+            for s in range(1, TAPS):
+                nc.vector.scalar_tensor_tensor(
+                    out=cv[:, :, s:FEAT],
+                    in0=o[:, 0, :, 0 : FEAT - s],
+                    scalar=taps[:, TAPS - 1 - s : TAPS - s],
+                    in1=cv[:, :, s:FEAT],
+                    op0=ALU.mult,
+                    op1=ALU.add,
+                )
+
+        def silu(g):
+            cv = conv_acc.pop(g)
+            xc = work.tile([P, SUB, FEAT], F32, name="xc")
+            nc.scalar.activation(out=xc[:], in_=cv[:], func=ACT.Silu)
+            nc.sync.dma_start(out=group_rows(out_1, g), in_=xc[:])
+
+        stats(0)
+        ln_cols, w_codes, w_scales, bias_bc, taps, cbias = constants()
+        for g in range(1, STATS_LEAD):
+            stats(g)
+        for step in range(N_GROUPS + 3):
+            banks = None
+            if 0 <= step - 1 < N_GROUPS:
+                transpose_and_scale(step - 1)
+            if 0 <= step - 2 < N_GROUPS:
+                banks = project(step - 2)
+            if step + STATS_LEAD < N_GROUPS:
+                stats(step + STATS_LEAD)
+            if step < N_GROUPS:
+                normalise(step)
+            if 0 <= step - 3 < N_GROUPS:
+                convolve(step - 3)
+                silu(step - 3)
+            if banks is not None:
+                add_bias(step - 2, banks)

@@ -18,7 +18,8 @@ EPS = 1e-5
 SUB = 4
 GROUP_ROWS = P * SUB
 N_GROUPS = ROWS // GROUP_ROWS
-STATS_LEAD = 3
+STATS_LEAD = 2
+SUB_ON_TENSOR = 3
 
 FLOPS = 2 * ROWS * IN * 2 * FEAT
 
@@ -33,7 +34,7 @@ def tile_mlstmblock_pa_t_kernel(
         small = ctx.enter_context(tc.tile_pool(name="small", bufs=STATS_LEAD + 3))
         work = ctx.enter_context(tc.tile_pool(name="work", bufs=3))
         tpsum = ctx.enter_context(tc.psum_pool(name="tpsum", bufs=1))
-        mpsum = ctx.enter_context(tc.psum_pool(name="mpsum", bufs=4))
+        mpsum = ctx.enter_context(tc.psum_pool(name="mpsum", bufs=2))
         ctx.enter_context(tc.manual_schedule())
 
         def group_rows(dram, g):
@@ -49,6 +50,9 @@ def tile_mlstmblock_pa_t_kernel(
         nc.scalar.dma_start(out=vec_rows[0:PACK, :], in_=ln_w.rearrange("(c p) -> c p", p=P))
         nc.scalar.dma_start(
             out=vec_rows[PACK : 2 * PACK, :], in_=ln_b.rearrange("(c p) -> c p", p=P)
+        )
+        nc.scalar.dma_start(
+            out=vec_rows[2 * PACK : 2 * PACK + 1, :], in_=upL_b.rearrange("(c p) -> c p", p=P)
         )
         w_raw = const.tile([P, PACK, 2 * FEAT], BF16, name="w_raw")
         nc.scalar.dma_start(
@@ -72,16 +76,23 @@ def tile_mlstmblock_pa_t_kernel(
 
         mean_var = {}
         normed = {}
+        t_banks = {}
+        planes_of = {}
         grouped = {}
-        outs = {}
-        conv_acc = {}
+        mx_words = {}
+        row_banks = {}
+        left_t_bank = {}
+        left_t = {}
+        conv_bank = {}
+        conv_last = {}
 
         def stats(g):
+            st = small.tile([P, SUB, 6], F32, name="st")
             mv = small.tile([P, SUB, 2], F32, name="mv")
             for j in range(SUB):
-                st = small.tile([P, 6], F32, name="st")
-                nc.vector.bn_stats(out=st[:], in_=x_sb[g][:, j, :])
-                nc.vector.bn_aggr(out=mv[:, j, :], in_=st[:])
+                nc.vector.bn_stats(out=st[:, j, :], in_=x_sb[g][:, j, :])
+            for j in range(SUB):
+                nc.vector.bn_aggr(out=mv[:, j, :], in_=st[:, j, :])
             mean_var[g] = mv
 
         def constants():
@@ -89,8 +100,8 @@ def tile_mlstmblock_pa_t_kernel(
             nc.vector.tensor_copy(out=vec_rows32[:], in_=vec_rows[:])
             vec_ps = tpsum.tile([P, GROUP_ROWS], F32, name="vec_ps", tag="tp0")
             nc.tensor.transpose(out=vec_ps[:, 0:P], in_=vec_rows32[:], identity=ident[:])
-            ln_cols = const.tile([P, 2 * PACK], F32, name="ln_cols")
-            nc.vector.tensor_copy(out=ln_cols[:], in_=vec_ps[:, 0 : 2 * PACK])
+            cols = const.tile([P, 2 * PACK + 1], F32, name="cols")
+            nc.vector.tensor_copy(out=cols[:], in_=vec_ps[:, 0 : 2 * PACK + 1])
             w_grouped = const.tile([P, 2 * FEAT, PACK], BF16, name="w_grouped", align_bytes=64)
             nc.vector.tensor_copy(out=w_grouped[:], in_=w_raw[:].rearrange("p c n -> p n c"))
             w_codes = const.tile([P, 2 * FEAT], U32, name="w_codes", align_bytes=64)
@@ -106,7 +117,38 @@ def tile_mlstmblock_pa_t_kernel(
             nc.vector.tensor_copy(out=taps[:], in_=taps_bf[:])
             cbias = const.tile([P, 1], F32, name="cbias")
             nc.vector.tensor_copy(out=cbias[:], in_=cbias_bf[:])
-            return ln_cols, w_codes, w_scales, bias_bc, taps, cbias
+            band = const.tile([P, FEAT], F32, name="band")
+            nc.vector.tensor_scalar(
+                out=band[:], in0=ident[:], scalar1=taps[:, TAPS - 1 : TAPS], scalar2=None, op0=ALU.mult
+            )
+            for s in range(1, TAPS):
+                nc.vector.scalar_tensor_tensor(
+                    out=band[:, s:FEAT],
+                    in0=ident[:, 0 : FEAT - s],
+                    scalar=taps[:, TAPS - 1 - s : TAPS - s],
+                    in1=band[:, s:FEAT],
+                    op0=ALU.mult,
+                    op1=ALU.add,
+                )
+            conv_of_bias = const.tile([P, FEAT], F32, name="conv_of_bias")
+            nc.vector.tensor_scalar(
+                out=conv_of_bias[:],
+                in0=bias_bc[:, 0:FEAT],
+                scalar1=taps[:, TAPS - 1 : TAPS],
+                scalar2=cbias[:, 0:1],
+                op0=ALU.mult,
+                op1=ALU.add,
+            )
+            for s in range(1, TAPS):
+                nc.vector.scalar_tensor_tensor(
+                    out=conv_of_bias[:, s:FEAT],
+                    in0=bias_bc[:, 0 : FEAT - s],
+                    scalar=taps[:, TAPS - 1 - s : TAPS - s],
+                    in1=conv_of_bias[:, s:FEAT],
+                    op0=ALU.mult,
+                    op1=ALU.add,
+                )
+            return cols, w_codes, w_scales, bias_bc, taps, cbias, band, conv_of_bias
 
         def normalise(g):
             mv = mean_var.pop(g)
@@ -114,12 +156,12 @@ def tile_mlstmblock_pa_t_kernel(
             nc.gpsimd.tensor_scalar(
                 out=var_eps[:], in0=mv[:, :, 1], scalar1=1.0, scalar2=EPS, op0=ALU.mult, op1=ALU.add
             )
-            rstd = small.tile([P, SUB], F32, name="rstd")
-            nc.gpsimd.tensor_tensor(out=rstd[:], in0=var_eps[:], in1=neg_half[:], op=ALU.pow)
             neg_mean = small.tile([P, SUB], F32, name="neg_mean")
             nc.gpsimd.tensor_scalar(
                 out=neg_mean[:], in0=mv[:, :, 0], scalar1=-1.0, scalar2=0.0, op0=ALU.mult, op1=ALU.add
             )
+            rstd = small.tile([P, SUB], F32, name="rstd")
+            nc.gpsimd.tensor_tensor(out=rstd[:], in0=var_eps[:], in1=neg_half[:], op=ALU.pow)
             t = work.tile([P, SUB, IN], F32, name="t")
             for j in range(SUB):
                 nc.gpsimd.tensor_scalar(
@@ -132,9 +174,8 @@ def tile_mlstmblock_pa_t_kernel(
                 )
             normed[g] = t
 
-        def transpose_and_scale(g):
+        def transpose(g):
             t = normed.pop(g)
-            planes = work.tile([P, PACK, GROUP_ROWS], BF16, name="planes")
             banks = []
             for c in range(PACK):
                 bank = tpsum.tile([P, GROUP_ROWS], F32, name="bank", tag="tp%d" % c)
@@ -145,19 +186,31 @@ def tile_mlstmblock_pa_t_kernel(
                         identity=ident[:],
                     )
                 banks.append(bank)
+            t_banks[g] = banks
+
+        def scale_shift(g):
+            banks = t_banks.pop(g)
+            planes = work.tile([P, PACK, GROUP_ROWS], BF16, name="planes")
             for c in range(PACK):
                 nc.scalar.activation(
                     out=planes[:, c, :],
                     in_=banks[c][:],
                     func=ACT.Identity,
-                    scale=ln_cols[:, c : c + 1],
-                    bias=ln_cols[:, PACK + c : PACK + c + 1],
+                    scale=cols[:, c : c + 1],
+                    bias=cols[:, PACK + c : PACK + c + 1],
                 )
+            planes_of[g] = planes
+
+        def regroup(g):
+            planes = planes_of.pop(g)
             grp = work.tile([P, GROUP_ROWS, PACK], BF16, name="grp", align_bytes=64)
-            nc.scalar.copy(out=grp[:], in_=planes[:].rearrange("p c r -> p r c"))
+            nc.scalar.copy(
+                out=grp[:].rearrange("p (q i) c -> p q c i", i=4),
+                in_=planes[:].rearrange("p c (q i) -> p q c i", i=4),
+            )
             grouped[g] = grp
 
-        def project(g):
+        def quantise(g):
             grp = grouped.pop(g)
             codes = work.tile([P, GROUP_ROWS], U32, name="codes", align_bytes=64)
             scales = work.tile([P, GROUP_ROWS], U8, name="scales", align_bytes=64)
@@ -166,84 +219,120 @@ def tile_mlstmblock_pa_t_kernel(
                 scales=scales[:],
                 in_=grp[:].rearrange("p r c -> p (r c)"),
             )
+            mx_words[g] = (codes, scales)
+
+        def project(g):
+            codes, scales = mx_words.pop(g)
             banks = []
             for h in range(SUB // 2):
                 acc = mpsum.tile([P, 2, 2 * FEAT], F32, name="acc")
                 for i in range(2):
-                    cols = slice((2 * h + i) * P, (2 * h + i + 1) * P)
+                    sub_cols = slice((2 * h + i) * P, (2 * h + i + 1) * P)
                     nc.tensor.matmul_mx(
                         out=acc[:, i, :],
-                        lhsT=codes[:, cols].bitcast(FP8X4),
-                        lhsT_scale=scales[:, cols],
+                        lhsT=codes[:, sub_cols].bitcast(FP8X4),
+                        lhsT_scale=scales[:, sub_cols],
                         rhs=w_codes[:].bitcast(FP8X4),
                         rhs_scale=w_scales[:],
                         start=True,
                         stop=True,
                     )
                 banks.append(acc)
-            return banks
-
-        def add_bias(g, banks):
-            o = work.tile([P, 2, SUB, FEAT], F32, name="o")
-            for h in range(SUB // 2):
-                nc.vector.tensor_tensor(
-                    out=o[:, :, 2 * h : 2 * h + 2, :].rearrange("p l j n -> p j l n"),
-                    in0=banks[h][:].rearrange("p j (l n) -> p j l n", l=2),
-                    in1=bias_bc[:]
-                    .rearrange("p (l n) -> p l n", l=2)
-                    .unsqueeze(1)
-                    .to_broadcast([P, 2, 2, FEAT]),
-                    op=ALU.add,
-                )
-            nc.sync.dma_start(out=group_rows(out_0, g), in_=o[:, 0, :, :])
-            nc.sync.dma_start(out=group_rows(out_2, g), in_=o[:, 1, :, :])
-            cv = work.tile([P, SUB, FEAT], F32, name="cv")
-            nc.gpsimd.tensor_scalar(
-                out=cv[:],
-                in0=o[:, 0, :, :],
-                scalar1=taps[:, TAPS - 1 : TAPS],
-                scalar2=cbias[:, 0:1],
-                op0=ALU.mult,
-                op1=ALU.add,
+            row_banks[g] = banks
+            lt = tpsum.tile([P, GROUP_ROWS], F32, name="lt")
+            nc.tensor.matmul_mx(
+                out=lt[:],
+                lhsT=w_codes[:, 0:FEAT].bitcast(FP8X4),
+                lhsT_scale=w_scales[:, 0:FEAT],
+                rhs=codes[:].bitcast(FP8X4),
+                rhs_scale=scales[:],
+                start=True,
+                stop=True,
             )
-            outs[g] = o
-            conv_acc[g] = cv
+            left_t_bank[g] = lt
 
-        def convolve(g):
-            o = outs.pop(g)
-            cv = conv_acc[g]
-            for s in range(1, TAPS):
+        def left_bias(g):
+            lt = left_t_bank.pop(g)
+            xlt = work.tile([P, GROUP_ROWS], F32, name="xlt")
+            nc.scalar.activation(
+                out=xlt[:], in_=lt[:], func=ACT.Identity, bias=cols[:, 2 * PACK : 2 * PACK + 1]
+            )
+            left_t[g] = xlt
+
+        def convolve_on_tensor(g):
+            xlt = left_t.pop(g)
+            cvp = tpsum.tile([P, SUB_ON_TENSOR, FEAT], F32, name="cvp")
+            for j in range(SUB_ON_TENSOR):
+                nc.tensor.matmul(
+                    out=cvp[:, j, :],
+                    lhsT=xlt[:, j * P : (j + 1) * P],
+                    rhs=band[:],
+                    start=True,
+                    stop=True,
+                )
+            conv_bank[g] = cvp
+
+        def add_bias_and_convolve_last(g):
+            banks = row_banks.pop(g)
+            o = work.tile([P, 2, SUB, FEAT], F32, name="o")
+            cv = work.tile([P, FEAT], F32, name="cv")
+            last_left = banks[SUB // 2 - 1][:, 1, 0:FEAT]
+            for s in range(TAPS):
                 nc.vector.scalar_tensor_tensor(
-                    out=cv[:, :, s:FEAT],
-                    in0=o[:, 0, :, 0 : FEAT - s],
+                    out=cv[:, s:FEAT],
+                    in0=last_left[:, 0 : FEAT - s],
                     scalar=taps[:, TAPS - 1 - s : TAPS - s],
-                    in1=cv[:, :, s:FEAT],
+                    in1=conv_of_bias[:] if s == 0 else cv[:, s:FEAT],
                     op0=ALU.mult,
                     op1=ALU.add,
                 )
+                if s < SUB // 2:
+                    nc.vector.tensor_tensor(
+                        out=o[:, :, 2 * s : 2 * s + 2, :].rearrange("p l j n -> p j l n"),
+                        in0=banks[s][:].rearrange("p j (l n) -> p j l n", l=2),
+                        in1=bias_bc[:]
+                        .rearrange("p (l n) -> p l n", l=2)
+                        .unsqueeze(1)
+                        .to_broadcast([P, 2, 2, FEAT]),
+                        op=ALU.add,
+                    )
+            nc.sync.dma_start(out=group_rows(out_0, g), in_=o[:, 0, :, :])
+            nc.sync.dma_start(out=group_rows(out_2, g), in_=o[:, 1, :, :])
+            conv_last[g] = cv
 
         def silu(g):
-            cv = conv_acc.pop(g)
+            cvp = conv_bank.pop(g)
+            cv = conv_last.pop(g)
             xc = work.tile([P, SUB, FEAT], F32, name="xc")
-            nc.scalar.activation(out=xc[:], in_=cv[:], func=ACT.Silu)
+            nc.scalar.activation(
+                out=xc[:, 0:SUB_ON_TENSOR, :], in_=cvp[:], func=ACT.Silu, bias=cbias[:, 0:1]
+            )
+            nc.scalar.activation(out=xc[:, SUB_ON_TENSOR, :], in_=cv[:], func=ACT.Silu)
             nc.sync.dma_start(out=group_rows(out_1, g), in_=xc[:])
 
         stats(0)
-        ln_cols, w_codes, w_scales, bias_bc, taps, cbias = constants()
+        cols, w_codes, w_scales, bias_bc, taps, cbias, band, conv_of_bias = constants()
         for g in range(1, STATS_LEAD):
             stats(g)
         for step in range(N_GROUPS + 3):
-            banks = None
-            if 0 <= step - 1 < N_GROUPS:
-                transpose_and_scale(step - 1)
-            if 0 <= step - 2 < N_GROUPS:
-                banks = project(step - 2)
+            late, mid, early = step - 3, step - 2, step - 1
+            if 0 <= late < N_GROUPS:
+                quantise(late)
+                project(late)
+            if 0 <= mid < N_GROUPS:
+                scale_shift(mid)
+            if 0 <= late < N_GROUPS:
+                left_bias(late)
+            if 0 <= mid < N_GROUPS:
+                regroup(mid)
+            if 0 <= early < N_GROUPS:
+                transpose(early)
+            if 0 <= late < N_GROUPS:
+                convolve_on_tensor(late)
             if step + STATS_LEAD < N_GROUPS:
                 stats(step + STATS_LEAD)
+            if 0 <= late < N_GROUPS:
+                add_bias_and_convolve_last(late)
+                silu(late)
             if step < N_GROUPS:
                 normalise(step)
-            if 0 <= step - 3 < N_GROUPS:
-                convolve(step - 3)
-                silu(step - 3)
-            if banks is not None:
-                add_bias(step - 2, banks)

@@ -20,6 +20,7 @@ GROUP_ROWS = P * SUB
 N_GROUPS = ROWS // GROUP_ROWS
 STATS_LEAD = 2
 SUB_ON_TENSOR = 3
+BANKS_ON_SCALAR = 3
 
 FLOPS = 2 * ROWS * IN * 2 * FEAT
 
@@ -93,7 +94,15 @@ def tile_mlstmblock_pa_t_kernel(
                 nc.vector.bn_stats(out=st[:, j, :], in_=x_sb[g][:, j, :])
             for j in range(SUB):
                 nc.vector.bn_aggr(out=mv[:, j, :], in_=st[:, j, :])
-            mean_var[g] = mv
+            var_eps = small.tile([P, SUB], F32, name="var_eps")
+            nc.vector.tensor_scalar(
+                out=var_eps[:], in0=mv[:, :, 1], scalar1=EPS, scalar2=None, op0=ALU.add
+            )
+            neg_mean = small.tile([P, SUB], F32, name="neg_mean")
+            nc.vector.tensor_scalar(
+                out=neg_mean[:], in0=mv[:, :, 0], scalar1=-1.0, scalar2=None, op0=ALU.mult
+            )
+            mean_var[g] = (neg_mean, var_eps)
 
         def constants():
             vec_rows32 = const.tile([P, P], F32, name="vec_rows32")
@@ -151,15 +160,7 @@ def tile_mlstmblock_pa_t_kernel(
             return cols, w_codes, w_scales, bias_bc, taps, cbias, band, conv_of_bias
 
         def normalise(g):
-            mv = mean_var.pop(g)
-            var_eps = small.tile([P, SUB], F32, name="var_eps")
-            nc.gpsimd.tensor_scalar(
-                out=var_eps[:], in0=mv[:, :, 1], scalar1=1.0, scalar2=EPS, op0=ALU.mult, op1=ALU.add
-            )
-            neg_mean = small.tile([P, SUB], F32, name="neg_mean")
-            nc.gpsimd.tensor_scalar(
-                out=neg_mean[:], in0=mv[:, :, 0], scalar1=-1.0, scalar2=0.0, op0=ALU.mult, op1=ALU.add
-            )
+            neg_mean, var_eps = mean_var.pop(g)
             rstd = small.tile([P, SUB], F32, name="rstd")
             nc.gpsimd.tensor_tensor(out=rstd[:], in0=var_eps[:], in1=neg_half[:], op=ALU.pow)
             t = work.tile([P, SUB, IN], F32, name="t")
@@ -191,7 +192,16 @@ def tile_mlstmblock_pa_t_kernel(
         def scale_shift(g):
             banks = t_banks.pop(g)
             planes = work.tile([P, PACK, GROUP_ROWS], BF16, name="planes")
-            for c in range(PACK):
+            for c in range(BANKS_ON_SCALAR, PACK):
+                nc.vector.tensor_scalar(
+                    out=planes[:, c, :],
+                    in0=banks[c][:],
+                    scalar1=cols[:, c : c + 1],
+                    scalar2=cols[:, PACK + c : PACK + c + 1],
+                    op0=ALU.mult,
+                    op1=ALU.add,
+                )
+            for c in range(BANKS_ON_SCALAR):
                 nc.scalar.activation(
                     out=planes[:, c, :],
                     in_=banks[c][:],

@@ -18,7 +18,6 @@ EPS = 1e-5
 SUB = 4
 GROUP_ROWS = P * SUB
 N_GROUPS = ROWS // GROUP_ROWS
-STATS_LEAD = 2
 SUB_ON_TENSOR = 3
 BANKS_ON_SCALAR = 3
 
@@ -32,11 +31,10 @@ def tile_mlstmblock_pa_t_kernel(
     with ExitStack() as ctx:
         const = ctx.enter_context(tc.tile_pool(name="const", bufs=1))
         xin = ctx.enter_context(tc.tile_pool(name="xin", bufs=1))
-        small = ctx.enter_context(tc.tile_pool(name="small", bufs=STATS_LEAD + 3))
+        small = ctx.enter_context(tc.tile_pool(name="small", bufs=4))
         work = ctx.enter_context(tc.tile_pool(name="work", bufs=3))
         tpsum = ctx.enter_context(tc.psum_pool(name="tpsum", bufs=1))
         mpsum = ctx.enter_context(tc.psum_pool(name="mpsum", bufs=2))
-        ctx.enter_context(tc.manual_schedule())
 
         def group_rows(dram, g):
             return dram[g * GROUP_ROWS : (g + 1) * GROUP_ROWS, :].rearrange(
@@ -177,16 +175,16 @@ def tile_mlstmblock_pa_t_kernel(
 
         def transpose(g):
             t = normed.pop(g)
-            banks = []
+            banks = [
+                tpsum.tile([P, GROUP_ROWS], F32, name="bank", tag="tp%d" % c) for c in range(PACK)
+            ]
             for c in range(PACK):
-                bank = tpsum.tile([P, GROUP_ROWS], F32, name="bank", tag="tp%d" % c)
                 for j in range(SUB):
                     nc.tensor.transpose(
-                        out=bank[:, j * P : (j + 1) * P],
+                        out=banks[c][:, j * P : (j + 1) * P],
                         in_=t[:, j, c * P : (c + 1) * P],
                         identity=ident[:],
                     )
-                banks.append(bank)
             t_banks[g] = banks
 
         def scale_shift(g):
@@ -322,27 +320,16 @@ def tile_mlstmblock_pa_t_kernel(
 
         stats(0)
         cols, w_codes, w_scales, bias_bc, taps, cbias, band, conv_of_bias = constants()
-        for g in range(1, STATS_LEAD):
-            stats(g)
-        for step in range(N_GROUPS + 3):
-            late, mid, early = step - 3, step - 2, step - 1
-            if 0 <= late < N_GROUPS:
-                quantise(late)
-                project(late)
-            if 0 <= mid < N_GROUPS:
-                scale_shift(mid)
-            if 0 <= late < N_GROUPS:
-                left_bias(late)
-            if 0 <= mid < N_GROUPS:
-                regroup(mid)
-            if 0 <= early < N_GROUPS:
-                transpose(early)
-            if 0 <= late < N_GROUPS:
-                convolve_on_tensor(late)
-            if step + STATS_LEAD < N_GROUPS:
-                stats(step + STATS_LEAD)
-            if 0 <= late < N_GROUPS:
-                add_bias_and_convolve_last(late)
-                silu(late)
-            if step < N_GROUPS:
-                normalise(step)
+        for g in range(N_GROUPS):
+            if g > 0:
+                stats(g)
+            normalise(g)
+            transpose(g)
+            scale_shift(g)
+            regroup(g)
+            quantise(g)
+            project(g)
+            left_bias(g)
+            convolve_on_tensor(g)
+            add_bias_and_convolve_last(g)
+            silu(g)

@@ -72,6 +72,8 @@ def tile_mlstmblock_pa_t_kernel(
         make_identity(nc, ident[:])
         neg_half = const.tile([P, SUB], F32, name="neg_half")
         nc.gpsimd.memset(neg_half[:], -0.5)
+        eps_col = const.tile([P, 1], F32, name="eps_col")
+        nc.gpsimd.memset(eps_col[:], EPS)
 
         mean_var = {}
         normed = {}
@@ -93,13 +95,9 @@ def tile_mlstmblock_pa_t_kernel(
             for j in range(SUB):
                 nc.vector.bn_aggr(out=mv[:, j, :], in_=st[:, j, :])
             var_eps = small.tile([P, SUB], F32, name="var_eps")
-            nc.vector.tensor_scalar(
-                out=var_eps[:], in0=mv[:, :, 1], scalar1=EPS, scalar2=None, op0=ALU.add
-            )
+            nc.scalar.activation(out=var_eps[:], in_=mv[:, :, 1], func=ACT.Identity, bias=eps_col[:, 0:1])
             neg_mean = small.tile([P, SUB], F32, name="neg_mean")
-            nc.vector.tensor_scalar(
-                out=neg_mean[:], in0=mv[:, :, 0], scalar1=-1.0, scalar2=None, op0=ALU.mult
-            )
+            nc.scalar.mul(out=neg_mean[:], in_=mv[:, :, 0], mul=-1.0)
             mean_var[g] = (neg_mean, var_eps)
 
         def constants():
@@ -261,9 +259,12 @@ def tile_mlstmblock_pa_t_kernel(
 
         def left_bias(g):
             lt = left_t_bank.pop(g)
-            xlt = work.tile([P, GROUP_ROWS], F32, name="xlt")
+            xlt = work.tile([P, SUB_ON_TENSOR * P], F32, name="xlt")
             nc.scalar.activation(
-                out=xlt[:], in_=lt[:], func=ACT.Identity, bias=cols[:, 2 * PACK : 2 * PACK + 1]
+                out=xlt[:],
+                in_=lt[:, 0 : SUB_ON_TENSOR * P],
+                func=ACT.Identity,
+                bias=cols[:, 2 * PACK : 2 * PACK + 1],
             )
             left_t[g] = xlt
 

from contextlib import ExitStack

import concourse.mybir as mybir
from concourse.masks import make_identity

F32 = mybir.dt.float32
BF16 = mybir.dt.bfloat16
U32 = mybir.dt.uint32
U8 = mybir.dt.uint8
FP8X4 = mybir.dt.float8_e4m3fn_x4
ALU = mybir.AluOpType
ACT = mybir.ActivationFunctionType

P = 128
PACK = 4
ROWS, IN, FEAT, TAPS = 8192, 512, 128, 4
EPS = 1e-5
SUB = 4
GROUP_ROWS = P * SUB
N_GROUPS = ROWS // GROUP_ROWS
SUB_ON_TENSOR = 3
BANKS_ON_SCALAR = 3

FLOPS = 2 * ROWS * IN * 2 * FEAT


def tile_mlstmblock_pa_t_kernel(
    tc, x, ln_w, ln_b, upL_w, upL_b, upR_w, upR_b, conv_w, conv_b, out_0, out_1, out_2
):
    nc = tc.nc
    with ExitStack() as ctx:
        const = ctx.enter_context(tc.tile_pool(name="const", bufs=1))
        xin = ctx.enter_context(tc.tile_pool(name="xin", bufs=1))
        small = ctx.enter_context(tc.tile_pool(name="small", bufs=4))
        work = ctx.enter_context(tc.tile_pool(name="work", bufs=3))
        tpsum = ctx.enter_context(tc.psum_pool(name="tpsum", bufs=1))
        mpsum = ctx.enter_context(tc.psum_pool(name="mpsum", bufs=2))

        def group_rows(dram, g):
            return dram[g * GROUP_ROWS : (g + 1) * GROUP_ROWS, :].rearrange(
                "(p j) n -> p j n", j=SUB
            )

        vec_rows = const.tile([P, P], BF16, name="vec_rows")
        nc.vector.memset(vec_rows[:], 0.0)
        x_sb = [xin.tile([P, SUB, IN], BF16, name="x%d" % g) for g in range(N_GROUPS)]
        for g in range(N_GROUPS):
            nc.sync.dma_start(out=x_sb[g][:], in_=group_rows(x, g))
        nc.scalar.dma_start(out=vec_rows[0:PACK, :], in_=ln_w.rearrange("(c p) -> c p", p=P))
        nc.scalar.dma_start(
            out=vec_rows[PACK : 2 * PACK, :], in_=ln_b.rearrange("(c p) -> c p", p=P)
        )
        nc.scalar.dma_start(
            out=vec_rows[2 * PACK : 2 * PACK + 1, :], in_=upL_b.rearrange("(c p) -> c p", p=P)
        )
        w_raw = const.tile([P, PACK, 2 * FEAT], BF16, name="w_raw")
        nc.scalar.dma_start(
            out=w_raw[:, :, 0:FEAT], in_=upL_w.rearrange("(c p) n -> p c n", p=P)
        )
        nc.scalar.dma_start(
            out=w_raw[:, :, FEAT : 2 * FEAT], in_=upR_w.rearrange("(c p) n -> p c n", p=P)
        )
        bias_bf = const.tile([P, 2 * FEAT], BF16, name="bias_bf")
        nc.scalar.dma_start(out=bias_bf[:, 0:FEAT], in_=upL_b.partition_broadcast(P))
        nc.scalar.dma_start(out=bias_bf[:, FEAT : 2 * FEAT], in_=upR_b.partition_broadcast(P))
        taps_bf = const.tile([P, TAPS], BF16, name="taps_bf")
        nc.scalar.dma_start(out=taps_bf[:], in_=conv_w.partition_broadcast(P))
        cbias_bf = const.tile([P, 1], BF16, name="cbias_bf")
        nc.scalar.dma_start(out=cbias_bf[:], in_=conv_b.partition_broadcast(P))

        ident = const.tile([P, P], F32, name="ident")
        make_identity(nc, ident[:])
        neg_half = const.tile([P, SUB], F32, name="neg_half")
        nc.gpsimd.memset(neg_half[:], -0.5)
        eps_col = const.tile([P, 1], F32, name="eps_col")
        nc.gpsimd.memset(eps_col[:], EPS)

        mean_var = {}
        normed = {}
        t_banks = {}
        planes_of = {}
        grouped = {}
        mx_words = {}
        row_banks = {}
        left_t_bank = {}
        left_t = {}
        conv_bank = {}
        conv_last = {}

        def stats(g):
            st = small.tile([P, SUB, 6], F32, name="st")
            mv = small.tile([P, SUB, 2], F32, name="mv")
            for j in range(SUB):
                nc.vector.bn_stats(out=st[:, j, :], in_=x_sb[g][:, j, :])
            for j in range(SUB):
                nc.vector.bn_aggr(out=mv[:, j, :], in_=st[:, j, :])
            var_eps = small.tile([P, SUB], F32, name="var_eps")
            nc.scalar.activation(out=var_eps[:], in_=mv[:, :, 1], func=ACT.Identity, bias=eps_col[:, 0:1])
            neg_mean = small.tile([P, SUB], F32, name="neg_mean")
            nc.scalar.mul(out=neg_mean[:], in_=mv[:, :, 0], mul=-1.0)
            mean_var[g] = (neg_mean, var_eps)

        def constants():
            vec_rows32 = const.tile([P, P], F32, name="vec_rows32")
            nc.vector.tensor_copy(out=vec_rows32[:], in_=vec_rows[:])
            vec_ps = tpsum.tile([P, GROUP_ROWS], F32, name="vec_ps", tag="tp0")
            nc.tensor.transpose(out=vec_ps[:, 0:P], in_=vec_rows32[:], identity=ident[:])
            cols = const.tile([P, 2 * PACK + 1], F32, name="cols")
            nc.vector.tensor_copy(out=cols[:], in_=vec_ps[:, 0 : 2 * PACK + 1])
            w_grouped = const.tile([P, 2 * FEAT, PACK], BF16, name="w_grouped", align_bytes=64)
            nc.vector.tensor_copy(out=w_grouped[:], in_=w_raw[:].rearrange("p c n -> p n c"))
            w_codes = const.tile([P, 2 * FEAT], U32, name="w_codes", align_bytes=64)
            w_scales = const.tile([P, 2 * FEAT], U8, name="w_scales", align_bytes=64)
            bias_bc = const.tile([P, 2 * FEAT], F32, name="bias_bc")
            nc.vector.tensor_copy(out=bias_bc[:], in_=bias_bf[:])
            nc.vector.quantize_mx(
                out=w_codes[:].bitcast(FP8X4),
                scales=w_scales[:],
                in_=w_grouped[:].rearrange("p n c -> p (n c)"),
            )
            taps = const.tile([P, TAPS], F32, name="taps")
            nc.vector.tensor_copy(out=taps[:], in_=taps_bf[:])
            cbias = const.tile([P, 1], F32, name="cbias")
            nc.vector.tensor_copy(out=cbias[:], in_=cbias_bf[:])
            band = const.tile([P, FEAT], F32, name="band")
            nc.vector.tensor_scalar(
                out=band[:], in0=ident[:], scalar1=taps[:, TAPS - 1 : TAPS], scalar2=None, op0=ALU.mult
            )
            for s in range(1, TAPS):
                nc.vector.scalar_tensor_tensor(
                    out=band[:, s:FEAT],
                    in0=ident[:, 0 : FEAT - s],
                    scalar=taps[:, TAPS - 1 - s : TAPS - s],
                    in1=band[:, s:FEAT],
                    op0=ALU.mult,
                    op1=ALU.add,
                )
            conv_of_bias = const.tile([P, FEAT], F32, name="conv_of_bias")
            nc.vector.tensor_scalar(
                out=conv_of_bias[:],
                in0=bias_bc[:, 0:FEAT],
                scalar1=taps[:, TAPS - 1 : TAPS],
                scalar2=cbias[:, 0:1],
                op0=ALU.mult,
                op1=ALU.add,
            )
            for s in range(1, TAPS):
                nc.vector.scalar_tensor_tensor(
                    out=conv_of_bias[:, s:FEAT],
                    in0=bias_bc[:, 0 : FEAT - s],
                    scalar=taps[:, TAPS - 1 - s : TAPS - s],
                    in1=conv_of_bias[:, s:FEAT],
                    op0=ALU.mult,
                    op1=ALU.add,
                )
            return cols, w_codes, w_scales, bias_bc, taps, cbias, band, conv_of_bias

        def normalise(g):
            neg_mean, var_eps = mean_var.pop(g)
            rstd = small.tile([P, SUB], F32, name="rstd")
            nc.gpsimd.tensor_tensor(out=rstd[:], in0=var_eps[:], in1=neg_half[:], op=ALU.pow)
            t = work.tile([P, SUB, IN], F32, name="t")
            for j in range(SUB):
                nc.gpsimd.tensor_scalar(
                    out=t[:, j, :],
                    in0=x_sb[g][:, j, :],
                    scalar1=neg_mean[:, j : j + 1],
                    scalar2=rstd[:, j : j + 1],
                    op0=ALU.add,
                    op1=ALU.mult,
                )
            normed[g] = t

        def transpose(g):
            t = normed.pop(g)
            banks = [
                tpsum.tile([P, GROUP_ROWS], F32, name="bank", tag="tp%d" % c) for c in range(PACK)
            ]
            for c in range(PACK):
                for j in range(SUB):
                    nc.tensor.transpose(
                        out=banks[c][:, j * P : (j + 1) * P],
                        in_=t[:, j, c * P : (c + 1) * P],
                        identity=ident[:],
                    )
            t_banks[g] = banks

        def scale_shift(g):
            banks = t_banks.pop(g)
            planes = work.tile([P, PACK, GROUP_ROWS], BF16, name="planes")
            for c in range(BANKS_ON_SCALAR, PACK):
                nc.vector.tensor_scalar(
                    out=planes[:, c, :],
                    in0=banks[c][:],
                    scalar1=cols[:, c : c + 1],
                    scalar2=cols[:, PACK + c : PACK + c + 1],
                    op0=ALU.mult,
                    op1=ALU.add,
                )
            for c in range(BANKS_ON_SCALAR):
                nc.scalar.activation(
                    out=planes[:, c, :],
                    in_=banks[c][:],
                    func=ACT.Identity,
                    scale=cols[:, c : c + 1],
                    bias=cols[:, PACK + c : PACK + c + 1],
                )
            planes_of[g] = planes

        def regroup(g):
            planes = planes_of.pop(g)
            grp = work.tile([P, GROUP_ROWS, PACK], BF16, name="grp", align_bytes=64)
            nc.scalar.copy(
                out=grp[:].rearrange("p (q i) c -> p q c i", i=4),
                in_=planes[:].rearrange("p c (q i) -> p q c i", i=4),
            )
            grouped[g] = grp

        def quantise(g):
            grp = grouped.pop(g)
            codes = work.tile([P, GROUP_ROWS], U32, name="codes", align_bytes=64)
            scales = work.tile([P, GROUP_ROWS], U8, name="scales", align_bytes=64)
            nc.vector.quantize_mx(
                out=codes[:].bitcast(FP8X4),
                scales=scales[:],
                in_=grp[:].rearrange("p r c -> p (r c)"),
            )
            mx_words[g] = (codes, scales)

        def project(g):
            codes, scales = mx_words.pop(g)
            banks = []
            for h in range(SUB // 2):
                acc = mpsum.tile([P, 2, 2 * FEAT], F32, name="acc")
                for i in range(2):
                    sub_cols = slice((2 * h + i) * P, (2 * h + i + 1) * P)
                    nc.tensor.matmul_mx(
                        out=acc[:, i, :],
                        lhsT=codes[:, sub_cols].bitcast(FP8X4),
                        lhsT_scale=scales[:, sub_cols],
                        rhs=w_codes[:].bitcast(FP8X4),
                        rhs_scale=w_scales[:],
                        start=True,
                        stop=True,
                    )
                banks.append(acc)
            row_banks[g] = banks
            lt = tpsum.tile([P, GROUP_ROWS], F32, name="lt")
            nc.tensor.matmul_mx(
                out=lt[:],
                lhsT=w_codes[:, 0:FEAT].bitcast(FP8X4),
                lhsT_scale=w_scales[:, 0:FEAT],
                rhs=codes[:].bitcast(FP8X4),
                rhs_scale=scales[:],
                start=True,
                stop=True,
            )
            left_t_bank[g] = lt

        def left_bias(g):
            lt = left_t_bank.pop(g)
            xlt = work.tile([P, SUB_ON_TENSOR * P], F32, name="xlt")
            nc.scalar.activation(
                out=xlt[:],
                in_=lt[:, 0 : SUB_ON_TENSOR * P],
                func=ACT.Identity,
                bias=cols[:, 2 * PACK : 2 * PACK + 1],
            )
            left_t[g] = xlt

        def convolve_on_tensor(g):
            xlt = left_t.pop(g)
            cvp = tpsum.tile([P, SUB_ON_TENSOR, FEAT], F32, name="cvp")
            for j in range(SUB_ON_TENSOR):
                nc.tensor.matmul(
                    out=cvp[:, j, :],
                    lhsT=xlt[:, j * P : (j + 1) * P],
                    rhs=band[:],
                    start=True,
                    stop=True,
                )
            conv_bank[g] = cvp

        def add_bias_and_convolve_last(g):
            banks = row_banks.pop(g)
            o = work.tile([P, 2, SUB, FEAT], F32, name="o")
            cv = work.tile([P, FEAT], F32, name="cv")
            last_left = banks[SUB // 2 - 1][:, 1, 0:FEAT]
            for s in range(TAPS):
                nc.vector.scalar_tensor_tensor(
                    out=cv[:, s:FEAT],
                    in0=last_left[:, 0 : FEAT - s],
                    scalar=taps[:, TAPS - 1 - s : TAPS - s],
                    in1=conv_of_bias[:] if s == 0 else cv[:, s:FEAT],
                    op0=ALU.mult,
                    op1=ALU.add,
                )
                if s < SUB // 2:
                    nc.vector.tensor_tensor(
                        out=o[:, :, 2 * s : 2 * s + 2, :].rearrange("p l j n -> p j l n"),
                        in0=banks[s][:].rearrange("p j (l n) -> p j l n", l=2),
                        in1=bias_bc[:]
                        .rearrange("p (l n) -> p l n", l=2)
                        .unsqueeze(1)
                        .to_broadcast([P, 2, 2, FEAT]),
                        op=ALU.add,
                    )
            nc.sync.dma_start(out=group_rows(out_0, g), in_=o[:, 0, :, :])
            nc.sync.dma_start(out=group_rows(out_2, g), in_=o[:, 1, :, :])
            conv_last[g] = cv

        def silu(g):
            cvp = conv_bank.pop(g)
            cv = conv_last.pop(g)
            xc = work.tile([P, SUB, FEAT], F32, name="xc")
            nc.scalar.activation(
                out=xc[:, 0:SUB_ON_TENSOR, :], in_=cvp[:], func=ACT.Silu, bias=cbias[:, 0:1]
            )
            nc.scalar.activation(out=xc[:, SUB_ON_TENSOR, :], in_=cv[:], func=ACT.Silu)
            nc.sync.dma_start(out=group_rows(out_1, g), in_=xc[:])

        stats(0)
        cols, w_codes, w_scales, bias_bc, taps, cbias, band, conv_of_bias = constants()
        for g in range(N_GROUPS):
            if g > 0:
                stats(g)
            normalise(g)
            transpose(g)
            scale_shift(g)
            regroup(g)
            quantise(g)
            project(g)
            left_bias(g)
            convolve_on_tensor(g)
            add_bias_and_convolve_last(g)
            silu(g)
